import numpy as np
import ml_dtypes

BF16 = ml_dtypes.bfloat16


def bf(x):
    return np.asarray(x, np.float32).astype(BF16)


def f32(x):
    return np.asarray(x, np.float32)


def f64(x):
    return np.asarray(x).astype(np.float64)


def striped(idx):
    return np.tile(idx.reshape(-1, 16).T, (8, 1))


D, S, H, H2, P, N = 128, 2048, 256, 512, 128, 2048
TEMP = 0.5


def sigmoid(v):
    return 1.0 / (1.0 + np.exp(-v))


def setup_inputs():
    return {
        "table": bf(np.random.standard_normal((D, S))),
        "wcn": bf(np.random.standard_normal((D, H)) / np.sqrt(D)),
        "bcn": f32(0.3 * np.random.standard_normal((H, 1))),
        "nb": f32(np.abs(np.random.standard_normal((H, N)))),
        "wnd": bf(np.random.standard_normal((H, H2)) / np.sqrt(H)),
        "bnd": f32(0.3 * np.random.standard_normal((H2, 1))),
        "wn3": bf(np.random.standard_normal((H2, P)) / np.sqrt(H2)),
        "bn3": f32(0.3 * np.random.standard_normal((P, 1))),
        "offs": striped(np.random.permutation(np.tile(np.arange(S), 2))[:N]),
    }


def reference(table, wcn, bcn, nb, wnd, bnd, wn3, bn3, offs):
    idx = offs[:16].T.reshape(-1)
    ctn = np.maximum(f64(wcn).T @ f64(table)[:, idx] + f64(bcn), 0.0)
    h = f64(nb) + ctn
    u = np.maximum(f64(wnd).T @ h + f64(bnd), 0.0)
    return sigmoid((f64(wn3).T @ u + f64(bn3)) / TEMP)

@@ -1,0 +1,103 @@
+import concourse.mybir as mybir
+
+BF16, F32, U16 = mybir.dt.bfloat16, mybir.dt.float32, mybir.dt.uint16
+ADD, MAX, MULT = mybir.AluOpType.add, mybir.AluOpType.max, mybir.AluOpType.mult
+RELU = mybir.ActivationFunctionType.Relu
+SIGMOID = mybir.ActivationFunctionType.Sigmoid
+
+P = 128
+S = 2048
+N = 2048
+H = 256
+H2 = 512
+PIECE = 512
+N_PIECES = N // PIECE
+H_BLOCKS = H // P
+U_BLOCKS = H2 // P
+OFFSET_COLUMNS = PIECE // 16
+
+FLOPS = 2 * N * (P * H + H * H2 + H2 * P)
+
+
+def tile_hier_node_vae_kernel(tc, table, wcn, bcn, nb, wnd, bnd, wn3, bn3, offs, out):
+    nc = tc.nc
+    with (
+        tc.tile_pool(name="held", bufs=1) as held,
+        tc.tile_pool(name="per_piece", bufs=N_PIECES) as per_piece,
+        tc.tile_pool(name="ring", bufs=4) as ring,
+        tc.psum_pool(name="banks", bufs=8) as banks,
+    ):
+        offsets = held.tile([P, N // 16], U16, name="offsets")
+        nc.sync.dma_start(offsets[:], offs)
+        table_sb = held.tile([P, S], BF16, name="table_sb")
+        nc.sync.dma_start(table_sb[:], table)
+        wcn_sb = held.tile([P, H], BF16, name="wcn_sb")
+        nc.scalar.dma_start(wcn_sb[:], wcn)
+
+        bcn_sb = held.tile([P, H_BLOCKS, 1], F32, name="bcn_sb")
+        wnd_sb = held.tile([P, H_BLOCKS, H2], BF16, name="wnd_sb")
+        bnd_sb = held.tile([P, U_BLOCKS, 1], F32, name="bnd_sb")
+        wn3_sb = held.tile([P, U_BLOCKS, P], BF16, name="wn3_sb")
+        bn3_sb = held.tile([P, 1], F32, name="bn3_sb")
+        with nc.allow_non_contiguous_dma(reason="a bias goes one element to a partition"):
+            nc.scalar.dma_start(bcn_sb[:], bcn.rearrange("(c p) o -> p c o", p=P))
+            nc.scalar.dma_start(wnd_sb[:], wnd.rearrange("(c p) e -> p c e", p=P))
+            nc.scalar.dma_start(bnd_sb[:], bnd.rearrange("(e p) o -> p e o", p=P))
+            nc.scalar.dma_start(wn3_sb[:], wn3.rearrange("(e p) q -> p e q", p=P))
+            nc.scalar.dma_start(bn3_sb[:], bn3)
+
+        bn3_doubled = held.tile([P, 1], F32, name="bn3_doubled")
+        nc.vector.tensor_scalar(bn3_doubled[:], bn3_sb[:], 2.0, None, MULT)
+
+        nb_blocks = nb.rearrange("(c p) n -> p c n", p=P)
+        h_pieces = []
+        for j in range(N_PIECES):
+            nodes = slice(j * PIECE, (j + 1) * PIECE)
+            nb_sb = per_piece.tile([P, H_BLOCKS, PIECE], F32, name="nb_sb")
+            nc.sync.dma_start(nb_sb[:], nb_blocks[:, :, nodes])
+            h = per_piece.tile([P, H_BLOCKS, PIECE], BF16, name="h")
+            h_pieces.append(h)
+            piece_offsets = offsets[:, j * OFFSET_COLUMNS : (j + 1) * OFFSET_COLUMNS]
+            for c in range(H_BLOCKS):
+                projected = banks.tile([P, PIECE], F32, name="projected", tag="bank")
+                nc.tensor.matmul(
+                    projected[:],
+                    wcn_sb[:, c * P : (c + 1) * P],
+                    table_sb[:].indirect(piece_offsets),
+                    start=True,
+                    stop=True,
+                )
+                ctn = ring.tile([P, PIECE], F32, name="ctn")
+                nc.scalar.activation(ctn[:], projected[:], RELU, bias=bcn_sb[:, c, :])
+                nc.vector.tensor_tensor(h[:, c, :], ctn[:], nb_sb[:, c, :], ADD)
+
+        for j in range(N_PIECES):
+            nodes = slice(j * PIECE, (j + 1) * PIECE)
+            h = h_pieces[j]
+            u = ring.tile([P, U_BLOCKS, PIECE], BF16, name="u")
+            for e in range(U_BLOCKS):
+                summed = banks.tile([P, PIECE], F32, name="summed", tag="bank")
+                for c in range(H_BLOCKS):
+                    nc.tensor.matmul(
+                        summed[:],
+                        wnd_sb[:, c, e * P : (e + 1) * P],
+                        h[:, c, :],
+                        start=(c == 0),
+                        stop=(c == H_BLOCKS - 1),
+                    )
+                if e % 2 == 0:
+                    nc.scalar.activation(u[:, e, :], summed[:], RELU, bias=bnd_sb[:, e, :])
+                else:
+                    nc.vector.tensor_scalar(u[:, e, :], summed[:], bnd_sb[:, e, :], 0.0, ADD, MAX)
+            logits = banks.tile([P, PIECE], F32, name="logits", tag="bank")
+            for e in range(U_BLOCKS):
+                nc.tensor.matmul(
+                    logits[:],
+                    wn3_sb[:, e, :],
+                    u[:, e, :],
+                    start=(e == 0),
+                    stop=(e == U_BLOCKS - 1),
+                )
+            y = ring.tile([P, PIECE], F32, name="y")
+            nc.scalar.activation(y[:], logits[:], SIGMOID, bias=bn3_doubled[:], scale=2.0)
+            nc.sync.dma_start(out[:, nodes], y[:])

@@ -15,6 +15,7 @@ N_PIECES = N // PIECE
 H_BLOCKS = H // P
 U_BLOCKS = H2 // P
 OFFSET_COLUMNS = PIECE // 16
+N_WARM = 8
 
 FLOPS = 2 * N * (P * H + H * H2 + H2 * P)
 
@@ -47,7 +48,15 @@ def tile_hier_node_vae_kernel(tc, table, wcn, bcn, nb, wnd, bnd, wn3, bn3, offs,
             nc.scalar.dma_start(bn3_sb[:], bn3)
 
         bn3_doubled = held.tile([P, 1], F32, name="bn3_doubled")
-        nc.vector.tensor_scalar(bn3_doubled[:], bn3_sb[:], 2.0, None, MULT)
+        nc.gpsimd.tensor_scalar(bn3_doubled[:], bn3_sb[:], 2.0, None, MULT)
+
+        zeros = held.tile([P, PIECE], BF16, name="zeros")
+        nc.vector.memset(zeros[:], 0.0)
+        warm_bank = banks.tile([P, PIECE], F32, name="warm_bank", tag="bank")
+        for i in range(N_WARM):
+            nc.tensor.matmul(warm_bank[:], zeros[:, 0:P], zeros[:], start=True, stop=True)
+        sigmoid_of_zero = held.tile([P, 1], F32, name="sigmoid_of_zero")
+        nc.scalar.activation(sigmoid_of_zero[:], zeros[:, 0:1], SIGMOID)
 
         nb_blocks = nb.rearrange("(c p) n -> p c n", p=P)
         h_pieces = []

@@ -15,7 +15,7 @@ N_PIECES = N // PIECE
 H_BLOCKS = H // P
 U_BLOCKS = H2 // P
 OFFSET_COLUMNS = PIECE // 16
-N_WARM = 8
+N_WARM = 5
 
 FLOPS = 2 * N * (P * H + H * H2 + H2 * P)
 
@@ -80,33 +80,37 @@ def tile_hier_node_vae_kernel(tc, table, wcn, bcn, nb, wnd, bnd, wn3, bn3, offs,
                 nc.scalar.activation(ctn[:], projected[:], RELU, bias=bcn_sb[:, c, :])
                 nc.vector.tensor_tensor(h[:, c, :], ctn[:], nb_sb[:, c, :], ADD)
 
-        for j in range(N_PIECES):
-            nodes = slice(j * PIECE, (j + 1) * PIECE)
-            h = h_pieces[j]
-            u = ring.tile([P, U_BLOCKS, PIECE], BF16, name="u")
-            for e in range(U_BLOCKS):
-                summed = banks.tile([P, PIECE], F32, name="summed", tag="bank")
-                for c in range(H_BLOCKS):
+        u_pieces = []
+        for j in range(N_PIECES + 1):
+            if j < N_PIECES:
+                h = h_pieces[j]
+                u = ring.tile([P, U_BLOCKS, PIECE], BF16, name="u")
+                u_pieces.append(u)
+                for e in range(U_BLOCKS):
+                    summed = banks.tile([P, PIECE], F32, name="summed", tag="bank")
+                    for c in range(H_BLOCKS):
+                        nc.tensor.matmul(
+                            summed[:],
+                            wnd_sb[:, c, e * P : (e + 1) * P],
+                            h[:, c, :],
+                            start=(c == 0),
+                            stop=(c == H_BLOCKS - 1),
+                        )
+                    if e % 2 == 0:
+                        nc.scalar.activation(u[:, e, :], summed[:], RELU, bias=bnd_sb[:, e, :])
+                    else:
+                        nc.vector.tensor_scalar(u[:, e, :], summed[:], bnd_sb[:, e, :], 0.0, ADD, MAX)
+            if j > 0:
+                u = u_pieces[j - 1]
+                logits = banks.tile([P, PIECE], F32, name="logits", tag="bank")
+                for e in range(U_BLOCKS):
                     nc.tensor.matmul(
-                        summed[:],
-                        wnd_sb[:, c, e * P : (e + 1) * P],
-                        h[:, c, :],
-                        start=(c == 0),
-                        stop=(c == H_BLOCKS - 1),
+                        logits[:],
+                        wn3_sb[:, e, :],
+                        u[:, e, :],
+                        start=(e == 0),
+                        stop=(e == U_BLOCKS - 1),
                     )
-                if e % 2 == 0:
-                    nc.scalar.activation(u[:, e, :], summed[:], RELU, bias=bnd_sb[:, e, :])
-                else:
-                    nc.vector.tensor_scalar(u[:, e, :], summed[:], bnd_sb[:, e, :], 0.0, ADD, MAX)
-            logits = banks.tile([P, PIECE], F32, name="logits", tag="bank")
-            for e in range(U_BLOCKS):
-                nc.tensor.matmul(
-                    logits[:],
-                    wn3_sb[:, e, :],
-                    u[:, e, :],
-                    start=(e == 0),
-                    stop=(e == U_BLOCKS - 1),
-                )
-            y = ring.tile([P, PIECE], F32, name="y")
-            nc.scalar.activation(y[:], logits[:], SIGMOID, bias=bn3_doubled[:], scale=2.0)
-            nc.sync.dma_start(out[:, nodes], y[:])
+                y = ring.tile([P, PIECE], F32, name="y")
+                nc.scalar.activation(y[:], logits[:], SIGMOID, bias=bn3_doubled[:], scale=2.0)
+                nc.sync.dma_start(out[:, (j - 1) * PIECE : j * PIECE], y[:])

@@ -28,42 +28,45 @@ def tile_hier_node_vae_kernel(tc, table, wcn, bcn, nb, wnd, bnd, wn3, bn3, offs,
         tc.tile_pool(name="ring", bufs=4) as ring,
         tc.psum_pool(name="banks", bufs=8) as banks,
     ):
+        zeros = held.tile([P, PIECE], BF16, name="zeros")
+        nc.gpsimd.memset(zeros[:], 0.0)
+        warm_bank = banks.tile([P, PIECE], F32, name="warm_bank", tag="bank")
+        for i in range(N_WARM):
+            nc.tensor.matmul(warm_bank[:], zeros[:, 0:P], zeros[:], start=True, stop=True)
+
+        table_sb = held.tile([P, S], BF16, name="table_sb")
+        nc.scalar.dma_start(table_sb[:], table)
         offsets = held.tile([P, N // 16], U16, name="offsets")
         nc.sync.dma_start(offsets[:], offs)
-        table_sb = held.tile([P, S], BF16, name="table_sb")
-        nc.sync.dma_start(table_sb[:], table)
         wcn_sb = held.tile([P, H], BF16, name="wcn_sb")
-        nc.scalar.dma_start(wcn_sb[:], wcn)
+        nc.sync.dma_start(wcn_sb[:], wcn)
+
+        sigmoid_of_zero = held.tile([P, 1], F32, name="sigmoid_of_zero")
+        nc.scalar.activation(sigmoid_of_zero[:], zeros[:, 0:1], SIGMOID)
 
         bcn_sb = held.tile([P, H_BLOCKS, 1], F32, name="bcn_sb")
         wnd_sb = held.tile([P, H_BLOCKS, H2], BF16, name="wnd_sb")
         bnd_sb = held.tile([P, U_BLOCKS, 1], F32, name="bnd_sb")
         wn3_sb = held.tile([P, U_BLOCKS, P], BF16, name="wn3_sb")
         bn3_sb = held.tile([P, 1], F32, name="bn3_sb")
+        nb_blocks = nb.rearrange("(c p) n -> p c n", p=P)
+        nb_pieces = [per_piece.tile([P, H_BLOCKS, PIECE], F32, name="nb_sb") for j in range(N_PIECES)]
         with nc.allow_non_contiguous_dma(reason="a bias goes one element to a partition"):
-            nc.scalar.dma_start(bcn_sb[:], bcn.rearrange("(c p) o -> p c o", p=P))
-            nc.scalar.dma_start(wnd_sb[:], wnd.rearrange("(c p) e -> p c e", p=P))
-            nc.scalar.dma_start(bnd_sb[:], bnd.rearrange("(e p) o -> p e o", p=P))
-            nc.scalar.dma_start(wn3_sb[:], wn3.rearrange("(e p) q -> p e q", p=P))
-            nc.scalar.dma_start(bn3_sb[:], bn3)
+            nc.sync.dma_start(bcn_sb[:], bcn.rearrange("(c p) o -> p c o", p=P))
+            nc.sync.dma_start(nb_pieces[0][:], nb_blocks[:, :, 0:PIECE])
+            nc.sync.dma_start(wnd_sb[:], wnd.rearrange("(c p) e -> p c e", p=P))
+            nc.sync.dma_start(bnd_sb[:], bnd.rearrange("(e p) o -> p e o", p=P))
+            for j in range(1, N_PIECES):
+                nc.sync.dma_start(nb_pieces[j][:], nb_blocks[:, :, j * PIECE : (j + 1) * PIECE])
+            nc.sync.dma_start(wn3_sb[:], wn3.rearrange("(e p) q -> p e q", p=P))
+            nc.sync.dma_start(bn3_sb[:], bn3)
 
         bn3_doubled = held.tile([P, 1], F32, name="bn3_doubled")
         nc.gpsimd.tensor_scalar(bn3_doubled[:], bn3_sb[:], 2.0, None, MULT)
 
-        zeros = held.tile([P, PIECE], BF16, name="zeros")
-        nc.vector.memset(zeros[:], 0.0)
-        warm_bank = banks.tile([P, PIECE], F32, name="warm_bank", tag="bank")
-        for i in range(N_WARM):
-            nc.tensor.matmul(warm_bank[:], zeros[:, 0:P], zeros[:], start=True, stop=True)
-        sigmoid_of_zero = held.tile([P, 1], F32, name="sigmoid_of_zero")
-        nc.scalar.activation(sigmoid_of_zero[:], zeros[:, 0:1], SIGMOID)
-
-        nb_blocks = nb.rearrange("(c p) n -> p c n", p=P)
         h_pieces = []
         for j in range(N_PIECES):
-            nodes = slice(j * PIECE, (j + 1) * PIECE)
-            nb_sb = per_piece.tile([P, H_BLOCKS, PIECE], F32, name="nb_sb")
-            nc.sync.dma_start(nb_sb[:], nb_blocks[:, :, nodes])
+            nb_sb = nb_pieces[j]
             h = per_piece.tile([P, H_BLOCKS, PIECE], BF16, name="h")
             h_pieces.append(h)
             piece_offsets = offsets[:, j * OFFSET_COLUMNS : (j + 1) * OFFSET_COLUMNS]

@@ -12,6 +12,7 @@ H = 256
 H2 = 512
 PIECE = 512
 N_PIECES = N // PIECE
+HALF = PIECE // 2
 H_BLOCKS = H // P
 U_BLOCKS = H2 // P
 OFFSET_COLUMNS = PIECE // 16
@@ -28,45 +29,42 @@ def tile_hier_node_vae_kernel(tc, table, wcn, bcn, nb, wnd, bnd, wn3, bn3, offs,
         tc.tile_pool(name="ring", bufs=4) as ring,
         tc.psum_pool(name="banks", bufs=8) as banks,
     ):
-        zeros = held.tile([P, PIECE], BF16, name="zeros")
-        nc.gpsimd.memset(zeros[:], 0.0)
-        warm_bank = banks.tile([P, PIECE], F32, name="warm_bank", tag="bank")
-        for i in range(N_WARM):
-            nc.tensor.matmul(warm_bank[:], zeros[:, 0:P], zeros[:], start=True, stop=True)
-
-        table_sb = held.tile([P, S], BF16, name="table_sb")
-        nc.scalar.dma_start(table_sb[:], table)
         offsets = held.tile([P, N // 16], U16, name="offsets")
         nc.sync.dma_start(offsets[:], offs)
+        table_sb = held.tile([P, S], BF16, name="table_sb")
+        nc.sync.dma_start(table_sb[:], table)
         wcn_sb = held.tile([P, H], BF16, name="wcn_sb")
-        nc.sync.dma_start(wcn_sb[:], wcn)
-
-        sigmoid_of_zero = held.tile([P, 1], F32, name="sigmoid_of_zero")
-        nc.scalar.activation(sigmoid_of_zero[:], zeros[:, 0:1], SIGMOID)
+        nc.scalar.dma_start(wcn_sb[:], wcn)
 
         bcn_sb = held.tile([P, H_BLOCKS, 1], F32, name="bcn_sb")
         wnd_sb = held.tile([P, H_BLOCKS, H2], BF16, name="wnd_sb")
         bnd_sb = held.tile([P, U_BLOCKS, 1], F32, name="bnd_sb")
         wn3_sb = held.tile([P, U_BLOCKS, P], BF16, name="wn3_sb")
         bn3_sb = held.tile([P, 1], F32, name="bn3_sb")
-        nb_blocks = nb.rearrange("(c p) n -> p c n", p=P)
-        nb_pieces = [per_piece.tile([P, H_BLOCKS, PIECE], F32, name="nb_sb") for j in range(N_PIECES)]
         with nc.allow_non_contiguous_dma(reason="a bias goes one element to a partition"):
-            nc.sync.dma_start(bcn_sb[:], bcn.rearrange("(c p) o -> p c o", p=P))
-            nc.sync.dma_start(nb_pieces[0][:], nb_blocks[:, :, 0:PIECE])
-            nc.sync.dma_start(wnd_sb[:], wnd.rearrange("(c p) e -> p c e", p=P))
-            nc.sync.dma_start(bnd_sb[:], bnd.rearrange("(e p) o -> p e o", p=P))
-            for j in range(1, N_PIECES):
-                nc.sync.dma_start(nb_pieces[j][:], nb_blocks[:, :, j * PIECE : (j + 1) * PIECE])
-            nc.sync.dma_start(wn3_sb[:], wn3.rearrange("(e p) q -> p e q", p=P))
-            nc.sync.dma_start(bn3_sb[:], bn3)
+            nc.scalar.dma_start(bcn_sb[:], bcn.rearrange("(c p) o -> p c o", p=P))
+            nc.scalar.dma_start(wnd_sb[:], wnd.rearrange("(c p) e -> p c e", p=P))
+            nc.scalar.dma_start(bnd_sb[:], bnd.rearrange("(e p) o -> p e o", p=P))
+            nc.scalar.dma_start(wn3_sb[:], wn3.rearrange("(e p) q -> p e q", p=P))
+            nc.scalar.dma_start(bn3_sb[:], bn3)
 
         bn3_doubled = held.tile([P, 1], F32, name="bn3_doubled")
         nc.gpsimd.tensor_scalar(bn3_doubled[:], bn3_sb[:], 2.0, None, MULT)
 
+        zeros = held.tile([P, PIECE], BF16, name="zeros")
+        nc.vector.memset(zeros[:], 0.0)
+        warm_bank = banks.tile([P, PIECE], F32, name="warm_bank", tag="bank")
+        for i in range(N_WARM):
+            nc.tensor.matmul(warm_bank[:], zeros[:, 0:P], zeros[:], start=True, stop=True)
+        sigmoid_of_zero = held.tile([P, 1], F32, name="sigmoid_of_zero")
+        nc.scalar.activation(sigmoid_of_zero[:], zeros[:, 0:1], SIGMOID)
+
+        nb_blocks = nb.rearrange("(c p) n -> p c n", p=P)
         h_pieces = []
         for j in range(N_PIECES):
-            nb_sb = nb_pieces[j]
+            nodes = slice(j * PIECE, (j + 1) * PIECE)
+            nb_sb = per_piece.tile([P, H_BLOCKS, PIECE], F32, name="nb_sb")
+            nc.sync.dma_start(nb_sb[:], nb_blocks[:, :, nodes])
             h = per_piece.tile([P, H_BLOCKS, PIECE], BF16, name="h")
             h_pieces.append(h)
             piece_offsets = offsets[:, j * OFFSET_COLUMNS : (j + 1) * OFFSET_COLUMNS]
@@ -105,15 +103,17 @@ def tile_hier_node_vae_kernel(tc, table, wcn, bcn, nb, wnd, bnd, wn3, bn3, offs,
                         nc.vector.tensor_scalar(u[:, e, :], summed[:], bnd_sb[:, e, :], 0.0, ADD, MAX)
             if j > 0:
                 u = u_pieces[j - 1]
-                logits = banks.tile([P, PIECE], F32, name="logits", tag="bank")
-                for e in range(U_BLOCKS):
-                    nc.tensor.matmul(
-                        logits[:],
-                        wn3_sb[:, e, :],
-                        u[:, e, :],
-                        start=(e == 0),
-                        stop=(e == U_BLOCKS - 1),
-                    )
-                y = ring.tile([P, PIECE], F32, name="y")
-                nc.scalar.activation(y[:], logits[:], SIGMOID, bias=bn3_doubled[:], scale=2.0)
-                nc.sync.dma_start(out[:, (j - 1) * PIECE : j * PIECE], y[:])
+                for first in range(0, PIECE, HALF):
+                    logits = banks.tile([P, HALF], F32, name="logits", tag="bank")
+                    for e in range(U_BLOCKS):
+                        nc.tensor.matmul(
+                            logits[:],
+                            wn3_sb[:, e, :],
+                            u[:, e, first : first + HALF],
+                            start=(e == 0),
+                            stop=(e == U_BLOCKS - 1),
+                        )
+                    y = ring.tile([P, HALF], F32, name="y")
+                    nc.scalar.activation(y[:], logits[:], SIGMOID, bias=bn3_doubled[:], scale=2.0)
+                    node = (j - 1) * PIECE + first
+                    nc.sync.dma_start(out[:, node : node + HALF], y[:])

@@ -16,7 +16,6 @@ HALF = PIECE // 2
 H_BLOCKS = H // P
 U_BLOCKS = H2 // P
 OFFSET_COLUMNS = PIECE // 16
-N_WARM = 5
 
 FLOPS = 2 * N * (P * H + H * H2 + H2 * P)
 
@@ -51,13 +50,10 @@ def tile_hier_node_vae_kernel(tc, table, wcn, bcn, nb, wnd, bnd, wn3, bn3, offs,
         bn3_doubled = held.tile([P, 1], F32, name="bn3_doubled")
         nc.gpsimd.tensor_scalar(bn3_doubled[:], bn3_sb[:], 2.0, None, MULT)
 
-        zeros = held.tile([P, PIECE], BF16, name="zeros")
+        zeros = held.tile([P, 1], F32, name="zeros")
         nc.vector.memset(zeros[:], 0.0)
-        warm_bank = banks.tile([P, PIECE], F32, name="warm_bank", tag="bank")
-        for i in range(N_WARM):
-            nc.tensor.matmul(warm_bank[:], zeros[:, 0:P], zeros[:], start=True, stop=True)
         sigmoid_of_zero = held.tile([P, 1], F32, name="sigmoid_of_zero")
-        nc.scalar.activation(sigmoid_of_zero[:], zeros[:, 0:1], SIGMOID)
+        nc.scalar.activation(sigmoid_of_zero[:], zeros[:], SIGMOID)
 
         nb_blocks = nb.rearrange("(c p) n -> p c n", p=P)
         h_pieces = []

@@ -28,10 +28,10 @@ def tile_hier_node_vae_kernel(tc, table, wcn, bcn, nb, wnd, bnd, wn3, bn3, offs,
         tc.tile_pool(name="ring", bufs=4) as ring,
         tc.psum_pool(name="banks", bufs=8) as banks,
     ):
-        offsets = held.tile([P, N // 16], U16, name="offsets")
-        nc.sync.dma_start(offsets[:], offs)
         table_sb = held.tile([P, S], BF16, name="table_sb")
         nc.sync.dma_start(table_sb[:], table)
+        offsets = held.tile([P, N // 16], U16, name="offsets")
+        nc.sync.dma_start(offsets[:], offs)
         wcn_sb = held.tile([P, H], BF16, name="wcn_sb")
         nc.scalar.dma_start(wcn_sb[:], wcn)
 
@@ -40,12 +40,18 @@ def tile_hier_node_vae_kernel(tc, table, wcn, bcn, nb, wnd, bnd, wn3, bn3, offs,
         bnd_sb = held.tile([P, U_BLOCKS, 1], F32, name="bnd_sb")
         wn3_sb = held.tile([P, U_BLOCKS, P], BF16, name="wn3_sb")
         bn3_sb = held.tile([P, 1], F32, name="bn3_sb")
+        nb_blocks = nb.rearrange("(c p) n -> p c n", p=P)
+        nb_pieces = []
         with nc.allow_non_contiguous_dma(reason="a bias goes one element to a partition"):
             nc.scalar.dma_start(bcn_sb[:], bcn.rearrange("(c p) o -> p c o", p=P))
-            nc.scalar.dma_start(wnd_sb[:], wnd.rearrange("(c p) e -> p c e", p=P))
             nc.scalar.dma_start(bnd_sb[:], bnd.rearrange("(e p) o -> p e o", p=P))
-            nc.scalar.dma_start(wn3_sb[:], wn3.rearrange("(e p) q -> p e q", p=P))
             nc.scalar.dma_start(bn3_sb[:], bn3)
+            nc.sync.dma_start(wnd_sb[:], wnd.rearrange("(c p) e -> p c e", p=P))
+            for j in range(N_PIECES):
+                nb_sb = per_piece.tile([P, H_BLOCKS, PIECE], F32, name="nb_sb")
+                nc.sync.dma_start(nb_sb[:], nb_blocks[:, :, j * PIECE : (j + 1) * PIECE])
+                nb_pieces.append(nb_sb)
+            nc.sync.dma_start(wn3_sb[:], wn3.rearrange("(e p) q -> p e q", p=P))
 
         bn3_doubled = held.tile([P, 1], F32, name="bn3_doubled")
         nc.gpsimd.tensor_scalar(bn3_doubled[:], bn3_sb[:], 2.0, None, MULT)
@@ -55,12 +61,9 @@ def tile_hier_node_vae_kernel(tc, table, wcn, bcn, nb, wnd, bnd, wn3, bn3, offs,
         sigmoid_of_zero = held.tile([P, 1], F32, name="sigmoid_of_zero")
         nc.scalar.activation(sigmoid_of_zero[:], zeros[:], SIGMOID)
 
-        nb_blocks = nb.rearrange("(c p) n -> p c n", p=P)
         h_pieces = []
         for j in range(N_PIECES):
-            nodes = slice(j * PIECE, (j + 1) * PIECE)
-            nb_sb = per_piece.tile([P, H_BLOCKS, PIECE], F32, name="nb_sb")
-            nc.sync.dma_start(nb_sb[:], nb_blocks[:, :, nodes])
+            nb_sb = nb_pieces[j]
             h = per_piece.tile([P, H_BLOCKS, PIECE], BF16, name="h")
             h_pieces.append(h)
             piece_offsets = offsets[:, j * OFFSET_COLUMNS : (j + 1) * OFFSET_COLUMNS]

@@ -12,7 +12,9 @@ H = 256
 H2 = 512
 PIECE = 512
 N_PIECES = N // PIECE
-HALF = PIECE // 2
+CHUNKS = (PIECE // 2, PIECE // 2)
+LAST_CHUNKS = (PIECE // 2, PIECE // 4, PIECE // 4)
+N_CHUNKS = (N_PIECES - 1) * len(CHUNKS) + len(LAST_CHUNKS)
 H_BLOCKS = H // P
 U_BLOCKS = H2 // P
 OFFSET_COLUMNS = PIECE // 16
@@ -26,6 +28,7 @@ def tile_hier_node_vae_kernel(tc, table, wcn, bcn, nb, wnd, bnd, wn3, bn3, offs,
         tc.tile_pool(name="held", bufs=1) as held,
         tc.tile_pool(name="per_piece", bufs=N_PIECES) as per_piece,
         tc.tile_pool(name="ring", bufs=4) as ring,
+        tc.tile_pool(name="outputs", bufs=N_CHUNKS) as outputs,
         tc.psum_pool(name="banks", bufs=8) as banks,
     ):
         table_sb = held.tile([P, S], BF16, name="table_sb")
@@ -102,17 +105,19 @@ def tile_hier_node_vae_kernel(tc, table, wcn, bcn, nb, wnd, bnd, wn3, bn3, offs,
                         nc.vector.tensor_scalar(u[:, e, :], summed[:], bnd_sb[:, e, :], 0.0, ADD, MAX)
             if j > 0:
                 u = u_pieces[j - 1]
-                for first in range(0, PIECE, HALF):
-                    logits = banks.tile([P, HALF], F32, name="logits", tag="bank")
+                node = (j - 1) * PIECE
+                first = 0
+                for width in CHUNKS if j < N_PIECES else LAST_CHUNKS:
+                    logits = banks.tile([P, width], F32, name="logits", tag="bank")
                     for e in range(U_BLOCKS):
                         nc.tensor.matmul(
                             logits[:],
                             wn3_sb[:, e, :],
-                            u[:, e, first : first + HALF],
+                            u[:, e, first : first + width],
                             start=(e == 0),
                             stop=(e == U_BLOCKS - 1),
                         )
-                    y = ring.tile([P, HALF], F32, name="y")
+                    y = outputs.tile([P, width], F32, name="y")
                     nc.scalar.activation(y[:], logits[:], SIGMOID, bias=bn3_doubled[:], scale=2.0)
-                    node = (j - 1) * PIECE + first
-                    nc.sync.dma_start(out[:, node : node + HALF], y[:])
+                    nc.sync.dma_start(out[:, node + first : node + first + width], y[:])
+                    first += width

@@ -47,14 +47,14 @@ def tile_hier_node_vae_kernel(tc, table, wcn, bcn, nb, wnd, bnd, wn3, bn3, offs,
         nb_pieces = []
         with nc.allow_non_contiguous_dma(reason="a bias goes one element to a partition"):
             nc.scalar.dma_start(bcn_sb[:], bcn.rearrange("(c p) o -> p c o", p=P))
-            nc.scalar.dma_start(bnd_sb[:], bnd.rearrange("(e p) o -> p e o", p=P))
+            nc.scalar.dma_start(bnd_sb[:], bnd.rearrange("(p e) o -> p e o", p=P))
             nc.scalar.dma_start(bn3_sb[:], bn3)
             nc.sync.dma_start(wnd_sb[:], wnd.rearrange("(c p) e -> p c e", p=P))
             for j in range(N_PIECES):
                 nb_sb = per_piece.tile([P, H_BLOCKS, PIECE], F32, name="nb_sb")
                 nc.sync.dma_start(nb_sb[:], nb_blocks[:, :, j * PIECE : (j + 1) * PIECE])
                 nb_pieces.append(nb_sb)
-            nc.sync.dma_start(wn3_sb[:], wn3.rearrange("(e p) q -> p e q", p=P))
+            nc.sync.dma_start(wn3_sb[:], wn3.rearrange("(p e) q -> p e q", p=P))
 
         bn3_doubled = held.tile([P, 1], F32, name="bn3_doubled")
         nc.gpsimd.tensor_scalar(bn3_doubled[:], bn3_sb[:], 2.0, None, MULT)
@@ -94,7 +94,7 @@ def tile_hier_node_vae_kernel(tc, table, wcn, bcn, nb, wnd, bnd, wn3, bn3, offs,
                     for c in range(H_BLOCKS):
                         nc.tensor.matmul(
                             summed[:],
-                            wnd_sb[:, c, e * P : (e + 1) * P],
+                            wnd_sb[:, c, e:H2:U_BLOCKS],
                             h[:, c, :],
                             start=(c == 0),
                             stop=(c == H_BLOCKS - 1),

@@ -43,13 +43,13 @@ def tile_hier_node_vae_kernel(tc, table, wcn, bcn, nb, wnd, bnd, wn3, bn3, offs,
         bnd_sb = held.tile([P, U_BLOCKS, 1], F32, name="bnd_sb")
         wn3_sb = held.tile([P, U_BLOCKS, P], BF16, name="wn3_sb")
         bn3_sb = held.tile([P, 1], F32, name="bn3_sb")
-        nb_blocks = nb.rearrange("(c p) n -> p c n", p=P)
+        nb_blocks = nb.rearrange("(p c) n -> p c n", p=P)
         nb_pieces = []
         with nc.allow_non_contiguous_dma(reason="a bias goes one element to a partition"):
-            nc.scalar.dma_start(bcn_sb[:], bcn.rearrange("(c p) o -> p c o", p=P))
+            nc.scalar.dma_start(bcn_sb[:], bcn.rearrange("(p c) o -> p c o", p=P))
             nc.scalar.dma_start(bnd_sb[:], bnd.rearrange("(p e) o -> p e o", p=P))
             nc.scalar.dma_start(bn3_sb[:], bn3)
-            nc.sync.dma_start(wnd_sb[:], wnd.rearrange("(c p) e -> p c e", p=P))
+            nc.sync.dma_start(wnd_sb[:], wnd.rearrange("(p c) e -> p c e", p=P))
             for j in range(N_PIECES):
                 nb_sb = per_piece.tile([P, H_BLOCKS, PIECE], F32, name="nb_sb")
                 nc.sync.dma_start(nb_sb[:], nb_blocks[:, :, j * PIECE : (j + 1) * PIECE])
@@ -74,7 +74,7 @@ def tile_hier_node_vae_kernel(tc, table, wcn, bcn, nb, wnd, bnd, wn3, bn3, offs,
                 projected = banks.tile([P, PIECE], F32, name="projected", tag="bank")
                 nc.tensor.matmul(
                     projected[:],
-                    wcn_sb[:, c * P : (c + 1) * P],
+                    wcn_sb[:, c:H:H_BLOCKS],
                     table_sb[:].indirect(piece_offsets),
                     start=True,
                     stop=True,

@@ -32,11 +32,11 @@ def tile_hier_node_vae_kernel(tc, table, wcn, bcn, nb, wnd, bnd, wn3, bn3, offs,
         tc.psum_pool(name="banks", bufs=8) as banks,
     ):
         table_sb = held.tile([P, S], BF16, name="table_sb")
-        nc.sync.dma_start(table_sb[:], table)
-        offsets = held.tile([P, N // 16], U16, name="offsets")
-        nc.sync.dma_start(offsets[:], offs)
         wcn_sb = held.tile([P, H], BF16, name="wcn_sb")
-        nc.scalar.dma_start(wcn_sb[:], wcn)
+        offsets = held.tile([P, N // 16], U16, name="offsets")
+        nc.sync.dma_start(table_sb[:], table)
+        nc.sync.dma_start(wcn_sb[:], wcn)
+        nc.sync.dma_start(offsets[:], offs)
 
         bcn_sb = held.tile([P, H_BLOCKS, 1], F32, name="bcn_sb")
         wnd_sb = held.tile([P, H_BLOCKS, H2], BF16, name="wnd_sb")
@@ -44,17 +44,21 @@ def tile_hier_node_vae_kernel(tc, table, wcn, bcn, nb, wnd, bnd, wn3, bn3, offs,
         wn3_sb = held.tile([P, U_BLOCKS, P], BF16, name="wn3_sb")
         bn3_sb = held.tile([P, 1], F32, name="bn3_sb")
         nb_blocks = nb.rearrange("(p c) n -> p c n", p=P)
-        nb_pieces = []
-        with nc.allow_non_contiguous_dma(reason="a bias goes one element to a partition"):
-            nc.scalar.dma_start(bcn_sb[:], bcn.rearrange("(p c) o -> p c o", p=P))
-            nc.scalar.dma_start(bnd_sb[:], bnd.rearrange("(p e) o -> p e o", p=P))
-            nc.scalar.dma_start(bn3_sb[:], bn3)
+        nb_pieces = [per_piece.tile([P, H_BLOCKS, PIECE], F32, name="nb_sb") for j in range(N_PIECES)]
+
+        def load_nb(j):
+            nc.sync.dma_start(nb_pieces[j][:], nb_blocks[:, :, j * PIECE : (j + 1) * PIECE])
+
+        with nc.allow_non_contiguous_dma(reason="a partition holds one to four elements of a bias"):
+            nc.sync.dma_start(bcn_sb[:], bcn.rearrange("(p c) o -> p c o", p=P))
+            load_nb(0)
             nc.sync.dma_start(wnd_sb[:], wnd.rearrange("(p c) e -> p c e", p=P))
-            for j in range(N_PIECES):
-                nb_sb = per_piece.tile([P, H_BLOCKS, PIECE], F32, name="nb_sb")
-                nc.sync.dma_start(nb_sb[:], nb_blocks[:, :, j * PIECE : (j + 1) * PIECE])
-                nb_pieces.append(nb_sb)
+            load_nb(1)
+            nc.sync.dma_start(bnd_sb[:], bnd.rearrange("(p e) o -> p e o", p=P))
+            load_nb(2)
             nc.sync.dma_start(wn3_sb[:], wn3.rearrange("(p e) q -> p e q", p=P))
+            nc.sync.dma_start(bn3_sb[:], bn3)
+            load_nb(3)
 
         bn3_doubled = held.tile([P, 1], F32, name="bn3_doubled")
         nc.gpsimd.tensor_scalar(bn3_doubled[:], bn3_sb[:], 2.0, None, MULT)

@@ -61,7 +61,7 @@ def tile_hier_node_vae_kernel(tc, table, wcn, bcn, nb, wnd, bnd, wn3, bn3, offs,
             load_nb(3)
 
         bn3_doubled = held.tile([P, 1], F32, name="bn3_doubled")
-        nc.gpsimd.tensor_scalar(bn3_doubled[:], bn3_sb[:], 2.0, None, MULT)
+        nc.vector.tensor_scalar(bn3_doubled[:], bn3_sb[:], 2.0, None, MULT)
 
         zeros = held.tile([P, 1], F32, name="zeros")
         nc.vector.memset(zeros[:], 0.0)

@@ -68,11 +68,8 @@ def tile_hier_node_vae_kernel(tc, table, wcn, bcn, nb, wnd, bnd, wn3, bn3, offs,
         sigmoid_of_zero = held.tile([P, 1], F32, name="sigmoid_of_zero")
         nc.scalar.activation(sigmoid_of_zero[:], zeros[:], SIGMOID)
 
-        h_pieces = []
-        for j in range(N_PIECES):
-            nb_sb = nb_pieces[j]
+        def project(j):
             h = per_piece.tile([P, H_BLOCKS, PIECE], BF16, name="h")
-            h_pieces.append(h)
             piece_offsets = offsets[:, j * OFFSET_COLUMNS : (j + 1) * OFFSET_COLUMNS]
             for c in range(H_BLOCKS):
                 projected = banks.tile([P, PIECE], F32, name="projected", tag="bank")
@@ -85,43 +82,54 @@ def tile_hier_node_vae_kernel(tc, table, wcn, bcn, nb, wnd, bnd, wn3, bn3, offs,
                 )
                 ctn = ring.tile([P, PIECE], F32, name="ctn")
                 nc.scalar.activation(ctn[:], projected[:], RELU, bias=bcn_sb[:, c, :])
-                nc.vector.tensor_tensor(h[:, c, :], ctn[:], nb_sb[:, c, :], ADD)
+                nc.vector.tensor_tensor(h[:, c, :], ctn[:], nb_pieces[j][:, c, :], ADD)
+            return h
 
-        u_pieces = []
-        for j in range(N_PIECES + 1):
-            if j < N_PIECES:
-                h = h_pieces[j]
-                u = ring.tile([P, U_BLOCKS, PIECE], BF16, name="u")
-                u_pieces.append(u)
+        def expand(h):
+            u = per_piece.tile([P, U_BLOCKS, PIECE], BF16, name="u")
+            for e in range(U_BLOCKS):
+                summed = banks.tile([P, PIECE], F32, name="summed", tag="bank")
+                for c in range(H_BLOCKS):
+                    nc.tensor.matmul(
+                        summed[:],
+                        wnd_sb[:, c, e:H2:U_BLOCKS],
+                        h[:, c, :],
+                        start=(c == 0),
+                        stop=(c == H_BLOCKS - 1),
+                    )
+                if e % 2 == 0:
+                    nc.scalar.activation(u[:, e, :], summed[:], RELU, bias=bnd_sb[:, e, :])
+                else:
+                    nc.vector.tensor_scalar(u[:, e, :], summed[:], bnd_sb[:, e, :], 0.0, ADD, MAX)
+            return u
+
+        def decode(j, u):
+            node = j * PIECE
+            first = 0
+            for width in LAST_CHUNKS if j == N_PIECES - 1 else CHUNKS:
+                logits = banks.tile([P, width], F32, name="logits", tag="bank")
                 for e in range(U_BLOCKS):
-                    summed = banks.tile([P, PIECE], F32, name="summed", tag="bank")
-                    for c in range(H_BLOCKS):
-                        nc.tensor.matmul(
-                            summed[:],
-                            wnd_sb[:, c, e:H2:U_BLOCKS],
-                            h[:, c, :],
-                            start=(c == 0),
-                            stop=(c == H_BLOCKS - 1),
-                        )
-                    if e % 2 == 0:
-                        nc.scalar.activation(u[:, e, :], summed[:], RELU, bias=bnd_sb[:, e, :])
-                    else:
-                        nc.vector.tensor_scalar(u[:, e, :], summed[:], bnd_sb[:, e, :], 0.0, ADD, MAX)
-            if j > 0:
-                u = u_pieces[j - 1]
-                node = (j - 1) * PIECE
-                first = 0
-                for width in CHUNKS if j < N_PIECES else LAST_CHUNKS:
-                    logits = banks.tile([P, width], F32, name="logits", tag="bank")
-                    for e in range(U_BLOCKS):
-                        nc.tensor.matmul(
-                            logits[:],
-                            wn3_sb[:, e, :],
-                            u[:, e, first : first + width],
-                            start=(e == 0),
-                            stop=(e == U_BLOCKS - 1),
-                        )
-                    y = outputs.tile([P, width], F32, name="y")
-                    nc.scalar.activation(y[:], logits[:], SIGMOID, bias=bn3_doubled[:], scale=2.0)
-                    nc.sync.dma_start(out[:, node + first : node + first + width], y[:])
-                    first += width
+                    nc.tensor.matmul(
+                        logits[:],
+                        wn3_sb[:, e, :],
+                        u[:, e, first : first + width],
+                        start=(e == 0),
+                        stop=(e == U_BLOCKS - 1),
+                    )
+                y = outputs.tile([P, width], F32, name="y")
+                nc.scalar.activation(y[:], logits[:], SIGMOID, bias=bn3_doubled[:], scale=2.0)
+                nc.sync.dma_start(out[:, node + first : node + first + width], y[:])
+                first += width
+
+        h0 = project(0)
+        h1 = project(1)
+        h2 = project(2)
+        u0 = expand(h0)
+        u1 = expand(h1)
+        decode(0, u0)
+        h3 = project(3)
+        u2 = expand(h2)
+        decode(1, u1)
+        u3 = expand(h3)
+        decode(2, u2)
+        decode(3, u3)

@@ -63,11 +63,6 @@ def tile_hier_node_vae_kernel(tc, table, wcn, bcn, nb, wnd, bnd, wn3, bn3, offs,
         bn3_doubled = held.tile([P, 1], F32, name="bn3_doubled")
         nc.vector.tensor_scalar(bn3_doubled[:], bn3_sb[:], 2.0, None, MULT)
 
-        zeros = held.tile([P, 1], F32, name="zeros")
-        nc.vector.memset(zeros[:], 0.0)
-        sigmoid_of_zero = held.tile([P, 1], F32, name="sigmoid_of_zero")
-        nc.scalar.activation(sigmoid_of_zero[:], zeros[:], SIGMOID)
-
         def project(j):
             h = per_piece.tile([P, H_BLOCKS, PIECE], BF16, name="h")
             piece_offsets = offsets[:, j * OFFSET_COLUMNS : (j + 1) * OFFSET_COLUMNS]

import concourse.mybir as mybir

BF16, F32, U16 = mybir.dt.bfloat16, mybir.dt.float32, mybir.dt.uint16
ADD, MAX, MULT = mybir.AluOpType.add, mybir.AluOpType.max, mybir.AluOpType.mult
RELU = mybir.ActivationFunctionType.Relu
SIGMOID = mybir.ActivationFunctionType.Sigmoid

P = 128
S = 2048
N = 2048
H = 256
H2 = 512
PIECE = 512
N_PIECES = N // PIECE
CHUNKS = (PIECE // 2, PIECE // 2)
LAST_CHUNKS = (PIECE // 2, PIECE // 4, PIECE // 4)
N_CHUNKS = (N_PIECES - 1) * len(CHUNKS) + len(LAST_CHUNKS)
H_BLOCKS = H // P
U_BLOCKS = H2 // P
OFFSET_COLUMNS = PIECE // 16

FLOPS = 2 * N * (P * H + H * H2 + H2 * P)


def tile_hier_node_vae_kernel(tc, table, wcn, bcn, nb, wnd, bnd, wn3, bn3, offs, out):
    nc = tc.nc
    with (
        tc.tile_pool(name="held", bufs=1) as held,
        tc.tile_pool(name="per_piece", bufs=N_PIECES) as per_piece,
        tc.tile_pool(name="ring", bufs=4) as ring,
        tc.tile_pool(name="outputs", bufs=N_CHUNKS) as outputs,
        tc.psum_pool(name="banks", bufs=8) as banks,
    ):
        table_sb = held.tile([P, S], BF16, name="table_sb")
        wcn_sb = held.tile([P, H], BF16, name="wcn_sb")
        offsets = held.tile([P, N // 16], U16, name="offsets")
        nc.sync.dma_start(table_sb[:], table)
        nc.sync.dma_start(wcn_sb[:], wcn)
        nc.sync.dma_start(offsets[:], offs)

        bcn_sb = held.tile([P, H_BLOCKS, 1], F32, name="bcn_sb")
        wnd_sb = held.tile([P, H_BLOCKS, H2], BF16, name="wnd_sb")
        bnd_sb = held.tile([P, U_BLOCKS, 1], F32, name="bnd_sb")
        wn3_sb = held.tile([P, U_BLOCKS, P], BF16, name="wn3_sb")
        bn3_sb = held.tile([P, 1], F32, name="bn3_sb")
        nb_blocks = nb.rearrange("(p c) n -> p c n", p=P)
        nb_pieces = [per_piece.tile([P, H_BLOCKS, PIECE], F32, name="nb_sb") for j in range(N_PIECES)]

        def load_nb(j):
            nc.sync.dma_start(nb_pieces[j][:], nb_blocks[:, :, j * PIECE : (j + 1) * PIECE])

        with nc.allow_non_contiguous_dma(reason="a partition holds one to four elements of a bias"):
            nc.sync.dma_start(bcn_sb[:], bcn.rearrange("(p c) o -> p c o", p=P))
            load_nb(0)
            nc.sync.dma_start(wnd_sb[:], wnd.rearrange("(p c) e -> p c e", p=P))
            load_nb(1)
            nc.sync.dma_start(bnd_sb[:], bnd.rearrange("(p e) o -> p e o", p=P))
            load_nb(2)
            nc.sync.dma_start(wn3_sb[:], wn3.rearrange("(p e) q -> p e q", p=P))
            nc.sync.dma_start(bn3_sb[:], bn3)
            load_nb(3)

        bn3_doubled = held.tile([P, 1], F32, name="bn3_doubled")
        nc.vector.tensor_scalar(bn3_doubled[:], bn3_sb[:], 2.0, None, MULT)

        def project(j):
            h = per_piece.tile([P, H_BLOCKS, PIECE], BF16, name="h")
            piece_offsets = offsets[:, j * OFFSET_COLUMNS : (j + 1) * OFFSET_COLUMNS]
            for c in range(H_BLOCKS):
                projected = banks.tile([P, PIECE], F32, name="projected", tag="bank")
                nc.tensor.matmul(
                    projected[:],
                    wcn_sb[:, c:H:H_BLOCKS],
                    table_sb[:].indirect(piece_offsets),
                    start=True,
                    stop=True,
                )
                ctn = ring.tile([P, PIECE], F32, name="ctn")
                nc.scalar.activation(ctn[:], projected[:], RELU, bias=bcn_sb[:, c, :])
                nc.vector.tensor_tensor(h[:, c, :], ctn[:], nb_pieces[j][:, c, :], ADD)
            return h

        def expand(h):
            u = per_piece.tile([P, U_BLOCKS, PIECE], BF16, name="u")
            for e in range(U_BLOCKS):
                summed = banks.tile([P, PIECE], F32, name="summed", tag="bank")
                for c in range(H_BLOCKS):
                    nc.tensor.matmul(
                        summed[:],
                        wnd_sb[:, c, e:H2:U_BLOCKS],
                        h[:, c, :],
                        start=(c == 0),
                        stop=(c == H_BLOCKS - 1),
                    )
                if e % 2 == 0:
                    nc.scalar.activation(u[:, e, :], summed[:], RELU, bias=bnd_sb[:, e, :])
                else:
                    nc.vector.tensor_scalar(u[:, e, :], summed[:], bnd_sb[:, e, :], 0.0, ADD, MAX)
            return u

        def decode(j, u):
            node = j * PIECE
            first = 0
            for width in LAST_CHUNKS if j == N_PIECES - 1 else CHUNKS:
                logits = banks.tile([P, width], F32, name="logits", tag="bank")
                for e in range(U_BLOCKS):
                    nc.tensor.matmul(
                        logits[:],
                        wn3_sb[:, e, :],
                        u[:, e, first : first + width],
                        start=(e == 0),
                        stop=(e == U_BLOCKS - 1),
                    )
                y = outputs.tile([P, width], F32, name="y")
                nc.scalar.activation(y[:], logits[:], SIGMOID, bias=bn3_doubled[:], scale=2.0)
                nc.sync.dma_start(out[:, node + first : node + first + width], y[:])
                first += width

        h0 = project(0)
        h1 = project(1)
        h2 = project(2)
        u0 = expand(h0)
        u1 = expand(h1)
        decode(0, u0)
        h3 = project(3)
        u2 = expand(h2)
        decode(1, u1)
        u3 = expand(h3)
        decode(2, u2)
        decode(3, u3)
